import numpy as np
import ml_dtypes


def mxq(x, axis, fmt="e4m3"):
    dtype, down = {"e4m3": (ml_dtypes.float8_e4m3fn, 7), "e5m2": (ml_dtypes.float8_e5m2, 14)}[fmt]
    v = np.moveaxis(np.asarray(x, np.float32).astype(ml_dtypes.bfloat16).astype(np.float64), axis, -1)
    blocks = v.reshape(v.shape[:-1] + (-1, 32))
    amax = np.abs(blocks).max(-1, keepdims=True)
    byte = np.maximum(np.where(amax > 0, np.frexp(amax)[1] - 1 + 127, 0) - down, 1)
    scale = np.exp2(byte - 127.0)
    codes = (blocks / scale).astype(np.float32).astype(dtype).astype(np.float64)
    return np.moveaxis((codes * scale).reshape(v.shape), -1, axis)


WIDE = False


def mx_kscale(k):
    if not WIDE:
        return np.ones(k)
    levels = np.array([10, -10, 5, -5, 0])
    a = np.random.permutation(np.resize(levels, k // 512 * 4)).reshape(k // 512, 4)
    idx = np.arange(k)
    return np.exp2(a[idx // 512, idx % 128 // 32])


BF16 = ml_dtypes.bfloat16


def bf(x):
    return np.asarray(x, np.float32).astype(BF16)


def f64(x):
    return np.asarray(x).astype(np.float64)


N, NQ, G, KW = 256, 1024, 3, 3
P = KW - 1


def x_taps(x):
    return np.moveaxis(x.reshape(N, NQ, G, P), -1, 0).swapaxes(-1, -2).reshape(P, N * G, NQ)


def q_rows(q):
    return q.swapaxes(-1, -2).reshape(N * G, NQ)


def conv(xq, qq, W, b):
    wt = W.transpose(2, 1, 0)
    return (xq @ mxq(wt[:P], 1, "e4m3")).sum(0) + (qq @ mxq(wt[P], 0, "e4m3")) + b


def setup_inputs():
    s = mx_kscale(NQ)
    w = 1.0 / np.sqrt(KW * NQ)
    return {"x": bf(np.random.standard_normal((N, NQ, G * P)) * s[None, :, None]),
            "q2": bf(np.maximum(np.random.standard_normal((N, NQ, G)) * 0.9, 0.0) * s[None, :, None]),
            "q1": bf(np.random.standard_normal((N, NQ, G))),
            "W3": bf(np.random.standard_normal((NQ, NQ, KW)) * w / s[None, :, None]),
            "b3": bf(np.random.standard_normal(NQ) * 0.2)}


def reference(x, q2, q1, W3, b3):
    y = conv(mxq(x_taps(f64(x)), 2, "e4m3"), mxq(q_rows(f64(q2)), 1, "e4m3"), f64(W3), f64(b3))
    return np.maximum(y.reshape(N, G, NQ).swapaxes(-1, -2) + f64(q1), 0.0)

@@ -1,0 +1,214 @@
+from contextlib import ExitStack
+
+import concourse.mybir as mybir
+from concourse.masks import make_identity
+
+FP8X4 = mybir.dt.float8_e4m3fn_x4
+BF16 = mybir.dt.bfloat16
+F32 = mybir.dt.float32
+U32 = mybir.dt.uint32
+U8 = mybir.dt.uint8
+ADD = mybir.AluOpType.add
+RELU = mybir.ActivationFunctionType.Relu
+
+P = 128
+N_ROWS, CH, GROUPS, TAPS = 256, 1024, 3, 3
+FLOPS = 2 * N_ROWS * GROUPS * CH * CH * TAPS
+
+ORDER = [("x", 0, 0), ("x", 0, 1), ("q", 0, 0), ("x", 1, 0), ("x", 1, 1), ("q", 1, 0), ("w", 0, 0), ("w", 1, 0), ("w", 2, 0), ("w", 3, 0), ("w", 4, 0), ("w", 5, 0), ("w", 6, 0), ("w", 7, 0)]
+D_ON_V = {"x": 2, "q": 3, "w": 2}
+E_ON_V = {"x": 0, "q": 0, "w": 0}
+Q1_POS = 6
+CAP = 2
+ACC_BUFS = 4
+MANUAL = True
+
+
+def tile_quadjetresnetblock_pb_kernel(tc, x, q2, q1, W3, b3, out):
+    nc = tc.nc
+    with ExitStack() as ctx:
+        if MANUAL:
+            ctx.enter_context(tc.manual_schedule())
+        const = ctx.enter_context(tc.tile_pool(name="const", bufs=1))
+        rawp = ctx.enter_context(tc.tile_pool(name="raw", bufs=1))
+        keep = ctx.enter_context(tc.tile_pool(name="keep", bufs=1))
+        dpool = ctx.enter_context(tc.tile_pool(name="dpool", bufs=3))
+        gpool = ctx.enter_context(tc.tile_pool(name="gpool", bufs=3))
+        tpsum = ctx.enter_context(tc.psum_pool(name="tpsum", bufs=4))
+        apsum = ctx.enter_context(tc.psum_pool(name="apsum", bufs=ACC_BUFS))
+
+        ident = const.tile([P, P], F32, name="ident")
+        make_identity(nc, ident[:])
+        bias = const.tile([P, CH], BF16, name="bias")
+
+        n_units = len(ORDER)
+        raw, codes, scales = {}, {}, {}
+        for u in ORDER:
+            raw[u] = rawp.tile([P, 3072], BF16, name="raw_%s%d%d" % u)
+            codes[u] = keep.tile([P, 768], U32, name="codes_%s%d%d" % u, align_bytes=64)
+            scales[u] = keep.tile([P, 768], U8, name="scales_%s%d%d" % u, align_bytes=64)
+        q1raw, resid = {}, {}
+        for i in range(2):
+            q1raw[i] = rawp.tile([P, 3072], BF16, name="q1raw_%d" % i)
+            resid[i] = keep.tile([P, 3072], F32, name="resid_%d" % i)
+
+        def rows(i):
+            return slice(P * i, P * (i + 1))
+
+        def load(u):
+            kind, a, b = u
+            if kind == "x":
+                src = x[rows(a), 512 * b:512 * (b + 1), :].rearrange("n c j -> n (c j)")
+            elif kind == "q":
+                src = q2[rows(a), :, :].rearrange("n c g -> n (c g)")
+            else:
+                src = W3[rows(a), :, :].rearrange("o c t -> o (c t)")
+            nc.sync.dma_start(out=raw[u][:], in_=src)
+
+        for k in range(n_units):
+            if k == Q1_POS:
+                nc.sync.dma_start(out=bias[:], in_=b3.partition_broadcast(P))
+                for i in range(2):
+                    nc.sync.dma_start(out=q1raw[i][:], in_=q1[rows(i), :, :].rearrange("n o g -> n (o g)"))
+            load(ORDER[k])
+
+        dtile, ptile, gtile, acc = {}, {}, {}, {}
+
+        def deinterleave(k):
+            u = ORDER[k]
+            d = dpool.tile([P, 6, 512], BF16, name="d", tag="d")
+            dtile[k] = d
+            if u[0] == "x":
+                src = raw[u][:].rearrange("p (c j) -> p j c", j=6)
+                dst = d[:]
+                step = 2
+            else:
+                src = raw[u][:].rearrange("p (c t) -> p t c", t=3)
+                dst = d[:].rearrange("p (t h) c -> p t (h c)", h=2)
+                step = 1
+            nv = D_ON_V[u[0]] * step
+            if nv > 0:
+                nc.vector.tensor_copy(out=dst[:, 0:nv, :], in_=src[:, 0:nv, :])
+            if nv < 3 * step:
+                nc.scalar.copy(out=dst[:, nv:3 * step, :], in_=src[:, nv:3 * step, :])
+
+        def transposes(k):
+            d = dtile[k]
+            ptile[k] = []
+            for b in range(3):
+                pt = tpsum.tile([P, 4, P], F32, name="pt", tag="pt")
+                ptile[k].append(pt)
+                for s2 in range(2):
+                    for w in range(2):
+                        nc.tensor.transpose(
+                            pt[:, 2 * s2 + w, :],
+                            d[:, 2 * b + s2, 256 * w:256 * (w + 1)].bitcast(F32),
+                            ident[:],
+                        )
+
+        def evacuate(k):
+            u = ORDER[k]
+            g = gpool.tile([P, 1536], F32, name="g", tag="g", align_bytes=64)
+            gtile[k] = g
+            for b in range(3):
+                dst = g[:, 512 * b:512 * (b + 1)].rearrange("p (s r w) -> p s r w", s=2, w=2)
+                src = ptile[k][b][:].rearrange("p (s w) r -> p s r w", w=2)
+                if b >= 3 - E_ON_V[u[0]]:
+                    nc.vector.tensor_copy(out=dst, in_=src)
+                else:
+                    nc.scalar.copy(out=dst, in_=src)
+
+        def quantise(k):
+            u = ORDER[k]
+            g = gtile[k]
+            for lo, hi in ((0, 512), (512, 768)):
+                nc.vector.quantize_mx(
+                    out=codes[u][:, lo:hi].bitcast(FP8X4),
+                    scales=scales[u][:, lo:hi],
+                    in_=g[:, 2 * lo:2 * hi].bitcast(BF16),
+                )
+
+        def sub(u, s):
+            cols = slice(P * s, P * (s + 1))
+            return codes[u][:, cols].bitcast(FP8X4), scales[u][:, cols]
+
+        def multiply(task):
+            i, j = task
+            a = apsum.tile([P, GROUPS, P], F32, name="acc", tag="acc")
+            acc[task] = a
+            for g in range(GROUPS):
+                n_pass = 0
+                for t in range(TAPS):
+                    for h in range(2):
+                        if t < 2:
+                            lc, ls = sub(("x", i, h), 2 * g + t)
+                        else:
+                            lc, ls = sub(("q", i, 0), 2 * g + h)
+                        rc, rs = sub(("w", j, 0), 2 * t + h)
+                        nc.tensor.matmul_mx(
+                            out=a[:, g, :], lhsT=lc, lhsT_scale=ls, rhs=rc, rhs_scale=rs,
+                            start=(n_pass == 0), stop=(n_pass == 5),
+                        )
+                        n_pass += 1
+
+        def piece(i, j):
+            return resid[i][:, 384 * j:384 * (j + 1)]
+
+        def residual(task):
+            i, j = task
+            nc.vector.tensor_tensor(
+                out=piece(i, j).rearrange("p (o g) -> p o g", g=GROUPS),
+                in0=q1raw[i][:, 384 * j:384 * (j + 1)].rearrange("p (o g) -> p o g", g=GROUPS),
+                in1=bias[:, P * j:P * (j + 1)].unsqueeze(2).to_broadcast([P, P, GROUPS]),
+                op=ADD,
+            )
+
+        def add(task):
+            i, j = task
+            view = piece(i, j).rearrange("p (o g) -> p o g", g=GROUPS)
+            nc.vector.tensor_tensor(out=view, in0=acc[task][:].rearrange("p g o -> p o g"), in1=view, op=ADD)
+
+        def relu_store(task):
+            i, j = task
+            nc.scalar.activation(out=piece(i, j), in_=piece(i, j), func=RELU)
+            nc.sync.dma_start(
+                out=out[rows(i), P * j:P * (j + 1), :].rearrange("n o g -> n (o g)"), in_=piece(i, j)
+            )
+
+        pos = {}
+        for k in range(n_units):
+            pos[ORDER[k]] = k
+        unlocked = [[] for k in range(n_units)]
+        for j in range(8):
+            for i in range(2):
+                last = max(pos[("x", i, 0)], pos[("x", i, 1)], pos[("q", i, 0)], pos[("w", j, 0)])
+                unlocked[last].append((i, j))
+
+        fifo, to_add = [], []
+        n_issued, n_added = 0, 0
+        for s in range(n_units + 12):
+            if 0 <= s - 2 < n_units:
+                quantise(s - 2)
+                fifo.extend(unlocked[s - 2])
+            to_relu = list(to_add)
+            for task in to_add:
+                add(task)
+                n_added += 1
+            to_add = []
+            if s < n_units:
+                deinterleave(s)
+            if 0 <= s - 1 < n_units:
+                transposes(s - 1)
+            n_now = 0
+            for task in fifo[n_issued:]:
+                if n_now >= CAP or n_issued - n_added >= ACC_BUFS:
+                    break
+                multiply(task)
+                residual(task)
+                to_add.append(task)
+                n_issued += 1
+                n_now += 1
+            if 0 <= s - 1 < n_units:
+                evacuate(s - 1)
+            for task in to_relu:
+                relu_store(task)

@@ -21,7 +21,7 @@ E_ON_V = {"x": 0, "q": 0, "w": 0}
 Q1_POS = 6
 CAP = 2
 ACC_BUFS = 4
-MANUAL = True
+MANUAL = False
 
 
 def tile_quadjetresnetblock_pb_kernel(tc, x, q2, q1, W3, b3, out):

@@ -16,26 +16,27 @@ N_ROWS, CH, GROUPS, TAPS = 256, 1024, 3, 3
 FLOPS = 2 * N_ROWS * GROUPS * CH * CH * TAPS
 
 ORDER = [("x", 0, 0), ("x", 0, 1), ("q", 0, 0), ("x", 1, 0), ("x", 1, 1), ("q", 1, 0), ("w", 0, 0), ("w", 1, 0), ("w", 2, 0), ("w", 3, 0), ("w", 4, 0), ("w", 5, 0), ("w", 6, 0), ("w", 7, 0)]
-D_ON_V = {"x": 2, "q": 3, "w": 2}
-E_ON_V = {"x": 0, "q": 0, "w": 0}
-Q1_POS = 6
-CAP = 2
-ACC_BUFS = 4
-MANUAL = False
+D_ON_V = [5,5,5,5,5,5,4,4,4,4,4,4,4,4]
+E_ON_V = [0,0,0,0,0,0,0,0,0,0,0,0,0,0]
+Q1_POS = 8
+SPLIT_FIRST = True
+TAIL_SPLIT = True
+S_E_FIRST = False
+N_PT = 4
+N_ACC = 4
+N_D = 3
+N_G = 3
 
 
 def tile_quadjetresnetblock_pb_kernel(tc, x, q2, q1, W3, b3, out):
     nc = tc.nc
     with ExitStack() as ctx:
-        if MANUAL:
-            ctx.enter_context(tc.manual_schedule())
+        ctx.enter_context(tc.manual_schedule())
         const = ctx.enter_context(tc.tile_pool(name="const", bufs=1))
         rawp = ctx.enter_context(tc.tile_pool(name="raw", bufs=1))
         keep = ctx.enter_context(tc.tile_pool(name="keep", bufs=1))
-        dpool = ctx.enter_context(tc.tile_pool(name="dpool", bufs=3))
-        gpool = ctx.enter_context(tc.tile_pool(name="gpool", bufs=3))
-        tpsum = ctx.enter_context(tc.psum_pool(name="tpsum", bufs=4))
-        apsum = ctx.enter_context(tc.psum_pool(name="apsum", bufs=ACC_BUFS))
+        work = ctx.enter_context(tc.tile_pool(name="work", bufs=1))
+        psum = ctx.enter_context(tc.psum_pool(name="psum", bufs=1))
 
         ident = const.tile([P, P], F32, name="ident")
         make_identity(nc, ident[:])
@@ -47,15 +48,15 @@ def tile_quadjetresnetblock_pb_kernel(tc, x, q2, q1, W3, b3, out):
             raw[u] = rawp.tile([P, 3072], BF16, name="raw_%s%d%d" % u)
             codes[u] = keep.tile([P, 768], U32, name="codes_%s%d%d" % u, align_bytes=64)
             scales[u] = keep.tile([P, 768], U8, name="scales_%s%d%d" % u, align_bytes=64)
-        q1raw, resid = {}, {}
-        for i in range(2):
-            q1raw[i] = rawp.tile([P, 3072], BF16, name="q1raw_%d" % i)
-            resid[i] = keep.tile([P, 3072], F32, name="resid_%d" % i)
+        q1raw = rawp.tile([P, 2, 3072], BF16, name="q1raw")
+        ep = {}
+        for j in range(8):
+            ep[j] = keep.tile([P, 2, 384], F32, name="ep%d" % j)
 
         def rows(i):
             return slice(P * i, P * (i + 1))
 
-        def load(u):
+        def load(u, split):
             kind, a, b = u
             if kind == "x":
                 src = x[rows(a), 512 * b:512 * (b + 1), :].rearrange("n c j -> n (c j)")
@@ -63,40 +64,58 @@ def tile_quadjetresnetblock_pb_kernel(tc, x, q2, q1, W3, b3, out):
                 src = q2[rows(a), :, :].rearrange("n c g -> n (c g)")
             else:
                 src = W3[rows(a), :, :].rearrange("o c t -> o (c t)")
-            nc.sync.dma_start(out=raw[u][:], in_=src)
+            if split:
+                nc.sync.dma_start(out=raw[u][:, 0:1536], in_=src[:, 0:1536])
+                nc.sync.dma_start(out=raw[u][:, 1536:3072], in_=src[:, 1536:3072])
+            else:
+                nc.sync.dma_start(out=raw[u][:], in_=src)
 
         for k in range(n_units):
             if k == Q1_POS:
                 nc.sync.dma_start(out=bias[:], in_=b3.partition_broadcast(P))
                 for i in range(2):
-                    nc.sync.dma_start(out=q1raw[i][:], in_=q1[rows(i), :, :].rearrange("n o g -> n (o g)"))
-            load(ORDER[k])
+                    nc.sync.dma_start(out=q1raw[:, i, :], in_=q1[rows(i), :, :].rearrange("n o g -> n (o g)"))
+            load(ORDER[k], SPLIT_FIRST and k == 0)
 
         dtile, ptile, gtile, acc = {}, {}, {}, {}
 
+        def copy_on(engine_is_vector, dst, src):
+            if engine_is_vector:
+                nc.vector.tensor_copy(out=dst, in_=src)
+            else:
+                nc.scalar.copy(out=dst, in_=src)
+
         def deinterleave(k):
             u = ORDER[k]
-            d = dpool.tile([P, 6, 512], BF16, name="d", tag="d")
+            d = work.tile([P, 6, 512], BF16, name="d%d" % (k % N_D), tag="d%d" % (k % N_D))
             dtile[k] = d
+            nv = D_ON_V[k]
             if u[0] == "x":
                 src = raw[u][:].rearrange("p (c j) -> p j c", j=6)
-                dst = d[:]
-                step = 2
+                halves = ((0, 256), (256, 512)) if (SPLIT_FIRST and k == 0) else ((0, 512),)
+                for lo, hi in halves:
+                    if nv > 0:
+                        copy_on(True, d[:, 0:nv, lo:hi], src[:, 0:nv, lo:hi])
+                    if nv < 6:
+                        copy_on(False, d[:, nv:6, lo:hi], src[:, nv:6, lo:hi])
             else:
-                src = raw[u][:].rearrange("p (c t) -> p t c", t=3)
-                dst = d[:].rearrange("p (t h) c -> p t (h c)", h=2)
-                step = 1
-            nv = D_ON_V[u[0]] * step
-            if nv > 0:
-                nc.vector.tensor_copy(out=dst[:, 0:nv, :], in_=src[:, 0:nv, :])
-            if nv < 3 * step:
-                nc.scalar.copy(out=dst[:, nv:3 * step, :], in_=src[:, nv:3 * step, :])
+                src = raw[u][:].rearrange("p (h c t) -> p t h c", h=2, t=3)
+                dst = d[:].rearrange("p (t h) c -> p t h c", h=2)
+                full = nv // 2
+                if full > 0:
+                    copy_on(True, dst[:, 0:full, :, :], src[:, 0:full, :, :])
+                if nv % 2 == 1:
+                    copy_on(True, dst[:, full, 0, :], src[:, full, 0, :])
+                    copy_on(False, dst[:, full, 1, :], src[:, full, 1, :])
+                    full += 1
+                if full < 3:
+                    copy_on(False, dst[:, full:3, :, :], src[:, full:3, :, :])
 
         def transposes(k):
             d = dtile[k]
             ptile[k] = []
             for b in range(3):
-                pt = tpsum.tile([P, 4, P], F32, name="pt", tag="pt")
+                pt = psum.tile([P, 4, P], F32, name="pt%d" % ((3 * k + b) % N_PT), tag="pt%d" % ((3 * k + b) % N_PT))
                 ptile[k].append(pt)
                 for s2 in range(2):
                     for w in range(2):
@@ -107,16 +126,12 @@ def tile_quadjetresnetblock_pb_kernel(tc, x, q2, q1, W3, b3, out):
                         )
 
         def evacuate(k):
-            u = ORDER[k]
-            g = gpool.tile([P, 1536], F32, name="g", tag="g", align_bytes=64)
+            g = work.tile([P, 1536], F32, name="g%d" % (k % N_G), tag="g%d" % (k % N_G), align_bytes=64)
             gtile[k] = g
             for b in range(3):
                 dst = g[:, 512 * b:512 * (b + 1)].rearrange("p (s r w) -> p s r w", s=2, w=2)
                 src = ptile[k][b][:].rearrange("p (s w) r -> p s r w", w=2)
-                if b >= 3 - E_ON_V[u[0]]:
-                    nc.vector.tensor_copy(out=dst, in_=src)
-                else:
-                    nc.scalar.copy(out=dst, in_=src)
+                copy_on(b >= 3 - E_ON_V[k], dst, src)
 
         def quantise(k):
             u = ORDER[k]
@@ -132,10 +147,9 @@ def tile_quadjetresnetblock_pb_kernel(tc, x, q2, q1, W3, b3, out):
             cols = slice(P * s, P * (s + 1))
             return codes[u][:, cols].bitcast(FP8X4), scales[u][:, cols]
 
-        def multiply(task):
-            i, j = task
-            a = apsum.tile([P, GROUPS, P], F32, name="acc", tag="acc")
-            acc[task] = a
+        def multiply(i, j):
+            a = psum.tile([P, GROUPS, P], F32, name="acc%d" % ((2 * j + i) % N_ACC), tag="acc%d" % ((2 * j + i) % N_ACC))
+            acc[(i, j)] = a
             for g in range(GROUPS):
                 n_pass = 0
                 for t in range(TAPS):
@@ -151,64 +165,56 @@ def tile_quadjetresnetblock_pb_kernel(tc, x, q2, q1, W3, b3, out):
                         )
                         n_pass += 1
 
-        def piece(i, j):
-            return resid[i][:, 384 * j:384 * (j + 1)]
-
-        def residual(task):
-            i, j = task
+        def residual(j):
             nc.vector.tensor_tensor(
-                out=piece(i, j).rearrange("p (o g) -> p o g", g=GROUPS),
-                in0=q1raw[i][:, 384 * j:384 * (j + 1)].rearrange("p (o g) -> p o g", g=GROUPS),
-                in1=bias[:, P * j:P * (j + 1)].unsqueeze(2).to_broadcast([P, P, GROUPS]),
+                out=ep[j][:].rearrange("p i (o g) -> p i o g", g=GROUPS),
+                in0=q1raw[:, :, 384 * j:384 * (j + 1)].rearrange("p i (o g) -> p i o g", g=GROUPS),
+                in1=bias[:, P * j:P * (j + 1)].unsqueeze(1).unsqueeze(3).to_broadcast([P, 2, P, GROUPS]),
                 op=ADD,
             )
 
-        def add(task):
-            i, j = task
-            view = piece(i, j).rearrange("p (o g) -> p o g", g=GROUPS)
-            nc.vector.tensor_tensor(out=view, in0=acc[task][:].rearrange("p g o -> p o g"), in1=view, op=ADD)
+        def add(i, j):
+            view = ep[j][:, i, :].rearrange("p (o g) -> p o g", g=GROUPS)
+            nc.vector.tensor_tensor(out=view, in0=acc[(i, j)][:].rearrange("p g o -> p o g"), in1=view, op=ADD)
 
-        def relu_store(task):
-            i, j = task
-            nc.scalar.activation(out=piece(i, j), in_=piece(i, j), func=RELU)
-            nc.sync.dma_start(
-                out=out[rows(i), P * j:P * (j + 1), :].rearrange("n o g -> n (o g)"), in_=piece(i, j)
-            )
+        out_v = out.rearrange("(i p) o g -> p i (o g)", p=P)
 
-        pos = {}
-        for k in range(n_units):
-            pos[ORDER[k]] = k
-        unlocked = [[] for k in range(n_units)]
-        for j in range(8):
-            for i in range(2):
-                last = max(pos[("x", i, 0)], pos[("x", i, 1)], pos[("q", i, 0)], pos[("w", j, 0)])
-                unlocked[last].append((i, j))
+        def relu_store(j):
+            if TAIL_SPLIT and j == 7:
+                for i in range(2):
+                    nc.scalar.activation(out=ep[j][:, i, :], in_=ep[j][:, i, :], func=RELU)
+                    nc.sync.dma_start(out=out_v[:, i, 384 * j:384 * (j + 1)], in_=ep[j][:, i, :])
+            else:
+                flat = ep[j][:].rearrange("p i c -> p (i c)")
+                nc.scalar.activation(out=flat, in_=flat, func=RELU)
+                nc.sync.dma_start(out=out_v[:, :, 384 * j:384 * (j + 1)], in_=ep[j][:])
 
-        fifo, to_add = [], []
-        n_issued, n_added = 0, 0
-        for s in range(n_units + 12):
+        first_w = n_units - 8
+        for s in range(n_units + 4):
             if 0 <= s - 2 < n_units:
                 quantise(s - 2)
-                fifo.extend(unlocked[s - 2])
-            to_relu = list(to_add)
-            for task in to_add:
-                add(task)
-                n_added += 1
-            to_add = []
-            if s < n_units:
-                deinterleave(s)
-            if 0 <= s - 1 < n_units:
-                transposes(s - 1)
-            n_now = 0
-            for task in fifo[n_issued:]:
-                if n_now >= CAP or n_issued - n_added >= ACC_BUFS:
-                    break
-                multiply(task)
-                residual(task)
-                to_add.append(task)
-                n_issued += 1
-                n_now += 1
-            if 0 <= s - 1 < n_units:
-                evacuate(s - 1)
-            for task in to_relu:
-                relu_store(task)
+            j_add = s - 3 - first_w
+            if 0 <= j_add < 8:
+                for i in range(2):
+                    add(i, j_add)
+            if S_E_FIRST:
+                if 0 <= s - 1 < n_units:
+                    transposes(s - 1)
+                    evacuate(s - 1)
+                if s < n_units:
+                    deinterleave(s)
+            else:
+                if s < n_units:
+                    deinterleave(s)
+                if 0 <= s - 1 < n_units:
+                    transposes(s - 1)
+            j_mul = s - 2 - first_w
+            if 0 <= j_mul < 8:
+                for i in range(2):
+                    multiply(i, j_mul)
+                residual(j_mul)
+            if not S_E_FIRST:
+                if 0 <= s - 1 < n_units:
+                    evacuate(s - 1)
+            if 0 <= j_add < 8:
+                relu_store(j_add)

@@ -16,7 +16,7 @@ N_ROWS, CH, GROUPS, TAPS = 256, 1024, 3, 3
 FLOPS = 2 * N_ROWS * GROUPS * CH * CH * TAPS
 
 ORDER = [("x", 0, 0), ("x", 0, 1), ("q", 0, 0), ("x", 1, 0), ("x", 1, 1), ("q", 1, 0), ("w", 0, 0), ("w", 1, 0), ("w", 2, 0), ("w", 3, 0), ("w", 4, 0), ("w", 5, 0), ("w", 6, 0), ("w", 7, 0)]
-D_ON_V = [5,5,5,5,5,5,4,4,4,4,4,4,4,4]
+D_ON_V = [416,416,416,416,416,416,320,320,320,320,320,320,320,320]
 E_ON_V = [0,0,0,0,0,0,0,0,0,0,0,0,0,0]
 Q1_POS = 8
 SPLIT_FIRST = True
@@ -89,27 +89,20 @@ def tile_quadjetresnetblock_pb_kernel(tc, x, q2, q1, W3, b3, out):
             u = ORDER[k]
             d = work.tile([P, 6, 512], BF16, name="d%d" % (k % N_D), tag="d%d" % (k % N_D))
             dtile[k] = d
-            nv = D_ON_V[k]
+            cv = D_ON_V[k]
             if u[0] == "x":
-                src = raw[u][:].rearrange("p (c j) -> p j c", j=6)
-                halves = ((0, 256), (256, 512)) if (SPLIT_FIRST and k == 0) else ((0, 512),)
-                for lo, hi in halves:
-                    if nv > 0:
-                        copy_on(True, d[:, 0:nv, lo:hi], src[:, 0:nv, lo:hi])
-                    if nv < 6:
-                        copy_on(False, d[:, nv:6, lo:hi], src[:, nv:6, lo:hi])
+                src = raw[u][:].rearrange("p (c a b) -> p a b c", a=2, b=3)
+                dst = d[:].rearrange("p (a b) c -> p a b c", a=2)
             else:
-                src = raw[u][:].rearrange("p (h c t) -> p t h c", h=2, t=3)
-                dst = d[:].rearrange("p (t h) c -> p t h c", h=2)
-                full = nv // 2
-                if full > 0:
-                    copy_on(True, dst[:, 0:full, :, :], src[:, 0:full, :, :])
-                if nv % 2 == 1:
-                    copy_on(True, dst[:, full, 0, :], src[:, full, 0, :])
-                    copy_on(False, dst[:, full, 1, :], src[:, full, 1, :])
-                    full += 1
-                if full < 3:
-                    copy_on(False, dst[:, full:3, :, :], src[:, full:3, :, :])
+                src = raw[u][:].rearrange("p (h c t) -> p h t c", h=2, t=3)
+                dst = d[:].rearrange("p (t h) c -> p h t c", h=2)
+            if SPLIT_FIRST and k == 0:
+                cuts = ((True, 0, 256), (True, 256, cv), (False, cv, 512))
+            else:
+                cuts = ((True, 0, cv), (False, cv, 512))
+            for on_vector, lo, hi in cuts:
+                if hi > lo:
+                    copy_on(on_vector, dst[:, :, :, lo:hi], src[:, :, :, lo:hi])
 
         def transposes(k):
             d = dtile[k]

@@ -15,13 +15,14 @@ P = 128
 N_ROWS, CH, GROUPS, TAPS = 256, 1024, 3, 3
 FLOPS = 2 * N_ROWS * GROUPS * CH * CH * TAPS
 
-ORDER = [("x", 0, 0), ("x", 0, 1), ("q", 0, 0), ("x", 1, 0), ("x", 1, 1), ("q", 1, 0), ("w", 0, 0), ("w", 1, 0), ("w", 2, 0), ("w", 3, 0), ("w", 4, 0), ("w", 5, 0), ("w", 6, 0), ("w", 7, 0)]
-D_ON_V = [416,416,416,416,416,416,320,320,320,320,320,320,320,320]
-E_ON_V = [0,0,0,0,0,0,0,0,0,0,0,0,0,0]
+ORDER = [("q", 0, 0), ("q", 1, 0), ("x", 0, 0), ("x", 0, 1), ("x", 1, 0), ("x", 1, 1), ("w", 0, 0), ("w", 1, 0), ("w", 2, 0), ("w", 3, 0), ("w", 4, 0), ("w", 5, 0), ("w", 6, 0), ("w", 7, 0)]
+D_ON_V = [352,384,0,0,0,0,352,320,320,320,320,320,320,320]
+E_ON_V = [0,0,2,1,1,1,0,0,0,0,0,0,0,1]
 Q1_POS = 8
 SPLIT_FIRST = True
 TAIL_SPLIT = True
 S_E_FIRST = False
+X_DIRECT = True
 N_PT = 4
 N_ACC = 4
 N_D = 3
@@ -87,6 +88,8 @@ def tile_quadjetresnetblock_pb_kernel(tc, x, q2, q1, W3, b3, out):
 
         def deinterleave(k):
             u = ORDER[k]
+            if X_DIRECT and u[0] == "x":
+                return
             d = work.tile([P, 6, 512], BF16, name="d%d" % (k % N_D), tag="d%d" % (k % N_D))
             dtile[k] = d
             cv = D_ON_V[k]
@@ -97,19 +100,34 @@ def tile_quadjetresnetblock_pb_kernel(tc, x, q2, q1, W3, b3, out):
                 src = raw[u][:].rearrange("p (h c t) -> p h t c", h=2, t=3)
                 dst = d[:].rearrange("p (t h) c -> p h t c", h=2)
             if SPLIT_FIRST and k == 0:
-                cuts = ((True, 0, 256), (True, 256, cv), (False, cv, 512))
-            else:
-                cuts = ((True, 0, cv), (False, cv, 512))
-            for on_vector, lo, hi in cuts:
+                for h in range(2):
+                    for on_vector, lo, hi in ((True, 0, cv), (False, cv, 512)):
+                        copy_on(
+                            on_vector,
+                            dst[:, h, :, lo:hi].rearrange("p t (a c) -> p a t c", a=2),
+                            src[:, h, :, lo:hi].rearrange("p t (a c) -> p a t c", a=2),
+                        )
+                return
+            for on_vector, lo, hi in ((True, 0, cv), (False, cv, 512)):
                 if hi > lo:
                     copy_on(on_vector, dst[:, :, :, lo:hi], src[:, :, :, lo:hi])
 
         def transposes(k):
-            d = dtile[k]
+            u = ORDER[k]
             ptile[k] = []
+            direct = X_DIRECT and u[0] == "x"
+            if direct:
+                words = raw[u][:].bitcast(F32).rearrange("p (w q e g) -> p w e g q", w=2, e=2, g=3)
+            else:
+                d = dtile[k]
             for b in range(3):
                 pt = psum.tile([P, 4, P], F32, name="pt%d" % ((3 * k + b) % N_PT), tag="pt%d" % ((3 * k + b) % N_PT))
                 ptile[k].append(pt)
+                if direct:
+                    for w in range(2):
+                        for e in range(2):
+                            nc.tensor.transpose(pt[:, 2 * w + e, :], words[:, w, e, b, :], ident[:])
+                    continue
                 for s2 in range(2):
                     for w in range(2):
                         nc.tensor.transpose(
@@ -121,9 +139,14 @@ def tile_quadjetresnetblock_pb_kernel(tc, x, q2, q1, W3, b3, out):
         def evacuate(k):
             g = work.tile([P, 1536], F32, name="g%d" % (k % N_G), tag="g%d" % (k % N_G), align_bytes=64)
             gtile[k] = g
+            direct = X_DIRECT and ORDER[k][0] == "x"
             for b in range(3):
-                dst = g[:, 512 * b:512 * (b + 1)].rearrange("p (s r w) -> p s r w", s=2, w=2)
-                src = ptile[k][b][:].rearrange("p (s w) r -> p s r w", w=2)
+                if direct:
+                    dst = g[:, 512 * b:512 * (b + 1)].bitcast(BF16).rearrange("p (t r v) -> p t r v", t=2, v=4)
+                    src = ptile[k][b][:].bitcast(BF16).rearrange("p v (r t) -> p t r v", t=2)
+                else:
+                    dst = g[:, 512 * b:512 * (b + 1)].rearrange("p (s r w) -> p s r w", s=2, w=2)
+                    src = ptile[k][b][:].rearrange("p (s w) r -> p s r w", w=2)
                 copy_on(b >= 3 - E_ON_V[k], dst, src)
 
         def quantise(k):

@@ -12,225 +12,208 @@ ADD = mybir.AluOpType.add
 RELU = mybir.ActivationFunctionType.Relu
 
 P = 128
-N_ROWS, CH, GROUPS, TAPS = 256, 1024, 3, 3
-FLOPS = 2 * N_ROWS * GROUPS * CH * CH * TAPS
+N_ROWS, CHANNELS, GROUPS, TAPS = 256, 1024, 3, 3
+ROW_TILES = N_ROWS // P
+W_TILES = CHANNELS // P
+K_PASS = 512
+HALVES = CHANNELS // K_PASS
+SIXTHS = 6
+UNIT = SIXTHS * K_PASS
+BANKS = 3
+FLOPS = 2 * N_ROWS * GROUPS * CHANNELS * CHANNELS * TAPS
 
-ORDER = [("q", 0, 0), ("q", 1, 0), ("x", 0, 0), ("x", 0, 1), ("x", 1, 0), ("x", 1, 1), ("w", 0, 0), ("w", 1, 0), ("w", 2, 0), ("w", 3, 0), ("w", 4, 0), ("w", 5, 0), ("w", 6, 0), ("w", 7, 0)]
-D_ON_V = [352,384,0,0,0,0,352,320,320,320,320,320,320,320]
-E_ON_V = [0,0,2,1,1,1,0,0,0,0,0,0,0,1]
-Q1_POS = 8
-SPLIT_FIRST = True
-TAIL_SPLIT = True
-S_E_FIRST = False
-X_DIRECT = True
-N_PT = 4
-N_ACC = 4
-N_D = 3
-N_G = 3
+UNITS = (
+    [("q2", i, 0) for i in range(ROW_TILES)]
+    + [("x", i, h) for i in range(ROW_TILES) for h in range(HALVES)]
+    + [("w", j, 0) for j in range(W_TILES)]
+)
+FIRST_W = len(UNITS) - W_TILES
+LOADS_BEFORE_RESIDUAL = FIRST_W + 2
+VECTOR_COLS = 352
+COPY_BUFS = 3
+GROUPED_BUFS = 3
+TRANSPOSE_BANKS = 4
+PRODUCT_BANKS = 4
 
 
 def tile_quadjetresnetblock_pb_kernel(tc, x, q2, q1, W3, b3, out):
     nc = tc.nc
     with ExitStack() as ctx:
         ctx.enter_context(tc.manual_schedule())
-        const = ctx.enter_context(tc.tile_pool(name="const", bufs=1))
-        rawp = ctx.enter_context(tc.tile_pool(name="raw", bufs=1))
-        keep = ctx.enter_context(tc.tile_pool(name="keep", bufs=1))
-        work = ctx.enter_context(tc.tile_pool(name="work", bufs=1))
+        fixed = ctx.enter_context(tc.tile_pool(name="fixed", bufs=1))
+        rotating = ctx.enter_context(tc.tile_pool(name="rotating", bufs=1))
         psum = ctx.enter_context(tc.psum_pool(name="psum", bufs=1))
 
-        ident = const.tile([P, P], F32, name="ident")
-        make_identity(nc, ident[:])
-        bias = const.tile([P, CH], BF16, name="bias")
-
-        n_units = len(ORDER)
-        raw, codes, scales = {}, {}, {}
-        for u in ORDER:
-            raw[u] = rawp.tile([P, 3072], BF16, name="raw_%s%d%d" % u)
-            codes[u] = keep.tile([P, 768], U32, name="codes_%s%d%d" % u, align_bytes=64)
-            scales[u] = keep.tile([P, 768], U8, name="scales_%s%d%d" % u, align_bytes=64)
-        q1raw = rawp.tile([P, 2, 3072], BF16, name="q1raw")
-        ep = {}
-        for j in range(8):
-            ep[j] = keep.tile([P, 2, 384], F32, name="ep%d" % j)
+        identity = fixed.tile([P, P], F32, name="identity")
+        make_identity(nc, identity[:])
+        bias = fixed.tile([P, CHANNELS], BF16, name="bias")
+        loaded, codes, scales = {}, {}, {}
+        for unit in UNITS:
+            loaded[unit] = fixed.tile([P, UNIT], BF16, name="loaded_%s%d%d" % unit)
+            codes[unit] = fixed.tile([P, UNIT // 4], U32, name="codes_%s%d%d" % unit, align_bytes=64)
+            scales[unit] = fixed.tile([P, UNIT // 4], U8, name="scales_%s%d%d" % unit, align_bytes=64)
+        q1_loaded = fixed.tile([P, ROW_TILES, GROUPS * CHANNELS], BF16, name="q1_loaded")
+        result = [fixed.tile([P, ROW_TILES, GROUPS * P], F32, name="result%d" % j) for j in range(W_TILES)]
 
         def rows(i):
             return slice(P * i, P * (i + 1))
 
-        def load(u, split):
-            kind, a, b = u
-            if kind == "x":
-                src = x[rows(a), 512 * b:512 * (b + 1), :].rearrange("n c j -> n (c j)")
-            elif kind == "q":
-                src = q2[rows(a), :, :].rearrange("n c g -> n (c g)")
-            else:
-                src = W3[rows(a), :, :].rearrange("o c t -> o (c t)")
-            if split:
-                nc.sync.dma_start(out=raw[u][:, 0:1536], in_=src[:, 0:1536])
-                nc.sync.dma_start(out=raw[u][:, 1536:3072], in_=src[:, 1536:3072])
-            else:
-                nc.sync.dma_start(out=raw[u][:], in_=src)
-
-        for k in range(n_units):
-            if k == Q1_POS:
+        for k, unit in enumerate(UNITS):
+            kind, i, h = unit
+            if k == LOADS_BEFORE_RESIDUAL:
                 nc.sync.dma_start(out=bias[:], in_=b3.partition_broadcast(P))
-                for i in range(2):
-                    nc.sync.dma_start(out=q1raw[:, i, :], in_=q1[rows(i), :, :].rearrange("n o g -> n (o g)"))
-            load(ORDER[k], SPLIT_FIRST and k == 0)
+                for r in range(ROW_TILES):
+                    nc.sync.dma_start(out=q1_loaded[:, r, :], in_=q1[rows(r), :, :].rearrange("n o g -> n (o g)"))
+            if kind == "x":
+                source = x[rows(i), K_PASS * h:K_PASS * (h + 1), :].rearrange("n c j -> n (c j)")
+            elif kind == "q2":
+                source = q2[rows(i), :, :].rearrange("n c g -> n (c g)")
+            else:
+                source = W3[rows(i), :, :].rearrange("o c t -> o (c t)")
+            if k == 0:
+                for half in range(HALVES):
+                    cols = slice(UNIT // 2 * half, UNIT // 2 * (half + 1))
+                    nc.sync.dma_start(out=loaded[unit][:, cols], in_=source[:, cols])
+            else:
+                nc.sync.dma_start(out=loaded[unit][:], in_=source)
 
-        dtile, ptile, gtile, acc = {}, {}, {}, {}
+        apart, transposed, grouped, product = {}, {}, {}, {}
 
-        def copy_on(engine_is_vector, dst, src):
-            if engine_is_vector:
+        def copy(on_vector, dst, src):
+            if on_vector:
                 nc.vector.tensor_copy(out=dst, in_=src)
             else:
                 nc.scalar.copy(out=dst, in_=src)
 
-        def deinterleave(k):
-            u = ORDER[k]
-            if X_DIRECT and u[0] == "x":
+        def set_taps_apart(k):
+            unit = UNITS[k]
+            if unit[0] == "x":
                 return
-            d = work.tile([P, 6, 512], BF16, name="d%d" % (k % N_D), tag="d%d" % (k % N_D))
-            dtile[k] = d
-            cv = D_ON_V[k]
-            if u[0] == "x":
-                src = raw[u][:].rearrange("p (c a b) -> p a b c", a=2, b=3)
-                dst = d[:].rearrange("p (a b) c -> p a b c", a=2)
-            else:
-                src = raw[u][:].rearrange("p (h c t) -> p h t c", h=2, t=3)
-                dst = d[:].rearrange("p (t h) c -> p h t c", h=2)
-            if SPLIT_FIRST and k == 0:
-                for h in range(2):
-                    for on_vector, lo, hi in ((True, 0, cv), (False, cv, 512)):
-                        copy_on(
+            tag = "apart%d" % (k % COPY_BUFS)
+            apart[k] = rotating.tile([P, SIXTHS, K_PASS], BF16, name=tag, tag=tag)
+            src = loaded[unit][:].rearrange("p (h c t) -> p h t c", h=HALVES, t=TAPS)
+            dst = apart[k][:].rearrange("p (t h) c -> p h t c", h=HALVES)
+            shares = ((True, 0, VECTOR_COLS), (False, VECTOR_COLS, K_PASS))
+            if k == 0:
+                for h in range(HALVES):
+                    for on_vector, lo, hi in shares:
+                        copy(
                             on_vector,
                             dst[:, h, :, lo:hi].rearrange("p t (a c) -> p a t c", a=2),
                             src[:, h, :, lo:hi].rearrange("p t (a c) -> p a t c", a=2),
                         )
-                return
-            for on_vector, lo, hi in ((True, 0, cv), (False, cv, 512)):
-                if hi > lo:
-                    copy_on(on_vector, dst[:, :, :, lo:hi], src[:, :, :, lo:hi])
-
-        def transposes(k):
-            u = ORDER[k]
-            ptile[k] = []
-            direct = X_DIRECT and u[0] == "x"
-            if direct:
-                words = raw[u][:].bitcast(F32).rearrange("p (w q e g) -> p w e g q", w=2, e=2, g=3)
             else:
-                d = dtile[k]
-            for b in range(3):
-                pt = psum.tile([P, 4, P], F32, name="pt%d" % ((3 * k + b) % N_PT), tag="pt%d" % ((3 * k + b) % N_PT))
-                ptile[k].append(pt)
-                if direct:
+                for on_vector, lo, hi in shares:
+                    copy(on_vector, dst[:, :, :, lo:hi], src[:, :, :, lo:hi])
+
+        def transpose(k):
+            unit = UNITS[k]
+            transposed[k] = []
+            for b in range(BANKS):
+                tag = "transposed%d" % ((BANKS * k + b) % TRANSPOSE_BANKS)
+                bank = psum.tile([P, 4, P], F32, name=tag, tag=tag)
+                transposed[k].append(bank)
+                if unit[0] == "x":
+                    words = loaded[unit][:].bitcast(F32).rearrange("r (w p e g) -> r w e g p", w=2, e=2, g=GROUPS)
                     for w in range(2):
                         for e in range(2):
-                            nc.tensor.transpose(pt[:, 2 * w + e, :], words[:, w, e, b, :], ident[:])
-                    continue
-                for s2 in range(2):
-                    for w in range(2):
-                        nc.tensor.transpose(
-                            pt[:, 2 * s2 + w, :],
-                            d[:, 2 * b + s2, 256 * w:256 * (w + 1)].bitcast(F32),
-                            ident[:],
-                        )
-
-        def evacuate(k):
-            g = work.tile([P, 1536], F32, name="g%d" % (k % N_G), tag="g%d" % (k % N_G), align_bytes=64)
-            gtile[k] = g
-            direct = X_DIRECT and ORDER[k][0] == "x"
-            for b in range(3):
-                if direct:
-                    dst = g[:, 512 * b:512 * (b + 1)].bitcast(BF16).rearrange("p (t r v) -> p t r v", t=2, v=4)
-                    src = ptile[k][b][:].bitcast(BF16).rearrange("p v (r t) -> p t r v", t=2)
+                            nc.tensor.transpose(bank[:, 2 * w + e, :], words[:, w, e, b, :], identity[:])
                 else:
-                    dst = g[:, 512 * b:512 * (b + 1)].rearrange("p (s r w) -> p s r w", s=2, w=2)
-                    src = ptile[k][b][:].rearrange("p (s w) r -> p s r w", w=2)
-                copy_on(b >= 3 - E_ON_V[k], dst, src)
+                    for s in range(2):
+                        for w in range(2):
+                            run = apart[k][:, 2 * b + s, 256 * w:256 * (w + 1)]
+                            nc.tensor.transpose(bank[:, 2 * s + w, :], run.bitcast(F32), identity[:])
+
+        def regroup(k):
+            unit = UNITS[k]
+            tag = "grouped%d" % (k % GROUPED_BUFS)
+            grouped[k] = rotating.tile([P, UNIT // 2], F32, name=tag, tag=tag, align_bytes=64)
+            for b in range(BANKS):
+                dst = grouped[k][:, 512 * b:512 * (b + 1)]
+                bank = transposed[k][b][:]
+                if unit[0] == "x":
+                    copy(
+                        b == BANKS - 1,
+                        dst.bitcast(BF16).rearrange("p (t r v) -> p t r v", t=2, v=4),
+                        bank.bitcast(BF16).rearrange("p v (r t) -> p t r v", t=2),
+                    )
+                else:
+                    copy(
+                        False,
+                        dst.rearrange("p (s r w) -> p s r w", s=2, w=2),
+                        bank.rearrange("p (s w) r -> p s r w", w=2),
+                    )
 
         def quantise(k):
-            u = ORDER[k]
-            g = gtile[k]
+            unit = UNITS[k]
             for lo, hi in ((0, 512), (512, 768)):
                 nc.vector.quantize_mx(
-                    out=codes[u][:, lo:hi].bitcast(FP8X4),
-                    scales=scales[u][:, lo:hi],
-                    in_=g[:, 2 * lo:2 * hi].bitcast(BF16),
+                    out=codes[unit][:, lo:hi].bitcast(FP8X4),
+                    scales=scales[unit][:, lo:hi],
+                    in_=grouped[k][:, 2 * lo:2 * hi].bitcast(BF16),
                 )
 
-        def sub(u, s):
-            cols = slice(P * s, P * (s + 1))
-            return codes[u][:, cols].bitcast(FP8X4), scales[u][:, cols]
+        def operand(unit, sixth):
+            cols = slice(P * sixth, P * (sixth + 1))
+            return codes[unit][:, cols].bitcast(FP8X4), scales[unit][:, cols]
 
         def multiply(i, j):
-            a = psum.tile([P, GROUPS, P], F32, name="acc%d" % ((2 * j + i) % N_ACC), tag="acc%d" % ((2 * j + i) % N_ACC))
-            acc[(i, j)] = a
+            tag = "product%d" % ((ROW_TILES * j + i) % PRODUCT_BANKS)
+            product[(i, j)] = psum.tile([P, GROUPS, P], F32, name=tag, tag=tag)
+            passes = [(t, h) for t in range(TAPS) for h in range(HALVES)]
             for g in range(GROUPS):
-                n_pass = 0
-                for t in range(TAPS):
-                    for h in range(2):
-                        if t < 2:
-                            lc, ls = sub(("x", i, h), 2 * g + t)
-                        else:
-                            lc, ls = sub(("q", i, 0), 2 * g + h)
-                        rc, rs = sub(("w", j, 0), 2 * t + h)
-                        nc.tensor.matmul_mx(
-                            out=a[:, g, :], lhsT=lc, lhsT_scale=ls, rhs=rc, rhs_scale=rs,
-                            start=(n_pass == 0), stop=(n_pass == 5),
-                        )
-                        n_pass += 1
+                for t, h in passes:
+                    if t < 2:
+                        a_codes, a_scales = operand(("x", i, h), 2 * g + t)
+                    else:
+                        a_codes, a_scales = operand(("q2", i, 0), HALVES * g + h)
+                    w_codes, w_scales = operand(("w", j, 0), HALVES * t + h)
+                    nc.tensor.matmul_mx(
+                        out=product[(i, j)][:, g, :],
+                        lhsT=a_codes,
+                        lhsT_scale=a_scales,
+                        rhs=w_codes,
+                        rhs_scale=w_scales,
+                        start=(t, h) == passes[0],
+                        stop=(t, h) == passes[-1],
+                    )
 
-        def residual(j):
+        def residual_plus_bias(j):
             nc.vector.tensor_tensor(
-                out=ep[j][:].rearrange("p i (o g) -> p i o g", g=GROUPS),
-                in0=q1raw[:, :, 384 * j:384 * (j + 1)].rearrange("p i (o g) -> p i o g", g=GROUPS),
-                in1=bias[:, P * j:P * (j + 1)].unsqueeze(1).unsqueeze(3).to_broadcast([P, 2, P, GROUPS]),
+                out=result[j][:].rearrange("p i (o g) -> p i o g", g=GROUPS),
+                in0=q1_loaded[:, :, GROUPS * P * j:GROUPS * P * (j + 1)].rearrange("p i (o g) -> p i o g", g=GROUPS),
+                in1=bias[:, P * j:P * (j + 1)].unsqueeze(1).unsqueeze(3).to_broadcast([P, ROW_TILES, P, GROUPS]),
                 op=ADD,
             )
 
-        def add(i, j):
-            view = ep[j][:, i, :].rearrange("p (o g) -> p o g", g=GROUPS)
-            nc.vector.tensor_tensor(out=view, in0=acc[(i, j)][:].rearrange("p g o -> p o g"), in1=view, op=ADD)
+        def add_product(i, j):
+            view = result[j][:, i, :].rearrange("p (o g) -> p o g", g=GROUPS)
+            nc.vector.tensor_tensor(out=view, in0=product[(i, j)][:].rearrange("p g o -> p o g"), in1=view, op=ADD)
 
-        out_v = out.rearrange("(i p) o g -> p i (o g)", p=P)
+        def relu_and_store(i, j):
+            nc.scalar.activation(out=result[j][:, i, :], in_=result[j][:, i, :], func=RELU)
+            nc.sync.dma_start(
+                out=out[rows(i), P * j:P * (j + 1), :].rearrange("n o g -> n (o g)"), in_=result[j][:, i, :]
+            )
 
-        def relu_store(j):
-            if TAIL_SPLIT and j == 7:
-                for i in range(2):
-                    nc.scalar.activation(out=ep[j][:, i, :], in_=ep[j][:, i, :], func=RELU)
-                    nc.sync.dma_start(out=out_v[:, i, 384 * j:384 * (j + 1)], in_=ep[j][:, i, :])
-            else:
-                flat = ep[j][:].rearrange("p i c -> p (i c)")
-                nc.scalar.activation(out=flat, in_=flat, func=RELU)
-                nc.sync.dma_start(out=out_v[:, :, 384 * j:384 * (j + 1)], in_=ep[j][:])
-
-        first_w = n_units - 8
-        for s in range(n_units + 4):
-            if 0 <= s - 2 < n_units:
-                quantise(s - 2)
-            j_add = s - 3 - first_w
-            if 0 <= j_add < 8:
-                for i in range(2):
-                    add(i, j_add)
-            if S_E_FIRST:
-                if 0 <= s - 1 < n_units:
-                    transposes(s - 1)
-                    evacuate(s - 1)
-                if s < n_units:
-                    deinterleave(s)
-            else:
-                if s < n_units:
-                    deinterleave(s)
-                if 0 <= s - 1 < n_units:
-                    transposes(s - 1)
-            j_mul = s - 2 - first_w
-            if 0 <= j_mul < 8:
-                for i in range(2):
-                    multiply(i, j_mul)
-                residual(j_mul)
-            if not S_E_FIRST:
-                if 0 <= s - 1 < n_units:
-                    evacuate(s - 1)
-            if 0 <= j_add < 8:
-                relu_store(j_add)
+        for step in range(len(UNITS) + 3):
+            multiplied = step - 2 - FIRST_W
+            finished = multiplied - 1
+            if 0 <= step - 2 < len(UNITS):
+                quantise(step - 2)
+            if 0 <= finished < W_TILES:
+                for i in range(ROW_TILES):
+                    add_product(i, finished)
+            if step < len(UNITS):
+                set_taps_apart(step)
+            if 0 <= step - 1 < len(UNITS):
+                transpose(step - 1)
+            if 0 <= multiplied < W_TILES:
+                for i in range(ROW_TILES):
+                    multiply(i, multiplied)
+                residual_plus_bias(multiplied)
+            if 0 <= step - 1 < len(UNITS):
+                regroup(step - 1)
+            if 0 <= finished < W_TILES:
+                for i in range(ROW_TILES):
+                    relu_and_store(i, finished)

@@ -29,7 +29,7 @@ UNITS = (
 )
 FIRST_W = len(UNITS) - W_TILES
 LOADS_BEFORE_RESIDUAL = FIRST_W + 2
-VECTOR_COLS = 352
+VECTOR_COLS = 416
 COPY_BUFS = 3
 GROUPED_BUFS = 3
 TRANSPOSE_BANKS = 4

from contextlib import ExitStack

import concourse.mybir as mybir
from concourse.masks import make_identity

FP8X4 = mybir.dt.float8_e4m3fn_x4
BF16 = mybir.dt.bfloat16
F32 = mybir.dt.float32
U32 = mybir.dt.uint32
U8 = mybir.dt.uint8
ADD = mybir.AluOpType.add
RELU = mybir.ActivationFunctionType.Relu

P = 128
N_ROWS, CHANNELS, GROUPS, TAPS = 256, 1024, 3, 3
ROW_TILES = N_ROWS // P
W_TILES = CHANNELS // P
K_PASS = 512
HALVES = CHANNELS // K_PASS
SIXTHS = 6
UNIT = SIXTHS * K_PASS
BANKS = 3
FLOPS = 2 * N_ROWS * GROUPS * CHANNELS * CHANNELS * TAPS

UNITS = (
    [("q2", i, 0) for i in range(ROW_TILES)]
    + [("x", i, h) for i in range(ROW_TILES) for h in range(HALVES)]
    + [("w", j, 0) for j in range(W_TILES)]
)
FIRST_W = len(UNITS) - W_TILES
LOADS_BEFORE_RESIDUAL = FIRST_W + 2
VECTOR_COLS = 416
COPY_BUFS = 3
GROUPED_BUFS = 3
TRANSPOSE_BANKS = 4
PRODUCT_BANKS = 4


def tile_quadjetresnetblock_pb_kernel(tc, x, q2, q1, W3, b3, out):
    nc = tc.nc
    with ExitStack() as ctx:
        ctx.enter_context(tc.manual_schedule())
        fixed = ctx.enter_context(tc.tile_pool(name="fixed", bufs=1))
        rotating = ctx.enter_context(tc.tile_pool(name="rotating", bufs=1))
        psum = ctx.enter_context(tc.psum_pool(name="psum", bufs=1))

        identity = fixed.tile([P, P], F32, name="identity")
        make_identity(nc, identity[:])
        bias = fixed.tile([P, CHANNELS], BF16, name="bias")
        loaded, codes, scales = {}, {}, {}
        for unit in UNITS:
            loaded[unit] = fixed.tile([P, UNIT], BF16, name="loaded_%s%d%d" % unit)
            codes[unit] = fixed.tile([P, UNIT // 4], U32, name="codes_%s%d%d" % unit, align_bytes=64)
            scales[unit] = fixed.tile([P, UNIT // 4], U8, name="scales_%s%d%d" % unit, align_bytes=64)
        q1_loaded = fixed.tile([P, ROW_TILES, GROUPS * CHANNELS], BF16, name="q1_loaded")
        result = [fixed.tile([P, ROW_TILES, GROUPS * P], F32, name="result%d" % j) for j in range(W_TILES)]

        def rows(i):
            return slice(P * i, P * (i + 1))

        for k, unit in enumerate(UNITS):
            kind, i, h = unit
            if k == LOADS_BEFORE_RESIDUAL:
                nc.sync.dma_start(out=bias[:], in_=b3.partition_broadcast(P))
                for r in range(ROW_TILES):
                    nc.sync.dma_start(out=q1_loaded[:, r, :], in_=q1[rows(r), :, :].rearrange("n o g -> n (o g)"))
            if kind == "x":
                source = x[rows(i), K_PASS * h:K_PASS * (h + 1), :].rearrange("n c j -> n (c j)")
            elif kind == "q2":
                source = q2[rows(i), :, :].rearrange("n c g -> n (c g)")
            else:
                source = W3[rows(i), :, :].rearrange("o c t -> o (c t)")
            if k == 0:
                for half in range(HALVES):
                    cols = slice(UNIT // 2 * half, UNIT // 2 * (half + 1))
                    nc.sync.dma_start(out=loaded[unit][:, cols], in_=source[:, cols])
            else:
                nc.sync.dma_start(out=loaded[unit][:], in_=source)

        apart, transposed, grouped, product = {}, {}, {}, {}

        def copy(on_vector, dst, src):
            if on_vector:
                nc.vector.tensor_copy(out=dst, in_=src)
            else:
                nc.scalar.copy(out=dst, in_=src)

        def set_taps_apart(k):
            unit = UNITS[k]
            if unit[0] == "x":
                return
            tag = "apart%d" % (k % COPY_BUFS)
            apart[k] = rotating.tile([P, SIXTHS, K_PASS], BF16, name=tag, tag=tag)
            src = loaded[unit][:].rearrange("p (h c t) -> p h t c", h=HALVES, t=TAPS)
            dst = apart[k][:].rearrange("p (t h) c -> p h t c", h=HALVES)
            shares = ((True, 0, VECTOR_COLS), (False, VECTOR_COLS, K_PASS))
            if k == 0:
                for h in range(HALVES):
                    for on_vector, lo, hi in shares:
                        copy(
                            on_vector,
                            dst[:, h, :, lo:hi].rearrange("p t (a c) -> p a t c", a=2),
                            src[:, h, :, lo:hi].rearrange("p t (a c) -> p a t c", a=2),
                        )
            else:
                for on_vector, lo, hi in shares:
                    copy(on_vector, dst[:, :, :, lo:hi], src[:, :, :, lo:hi])

        def transpose(k):
            unit = UNITS[k]
            transposed[k] = []
            for b in range(BANKS):
                tag = "transposed%d" % ((BANKS * k + b) % TRANSPOSE_BANKS)
                bank = psum.tile([P, 4, P], F32, name=tag, tag=tag)
                transposed[k].append(bank)
                if unit[0] == "x":
                    words = loaded[unit][:].bitcast(F32).rearrange("r (w p e g) -> r w e g p", w=2, e=2, g=GROUPS)
                    for w in range(2):
                        for e in range(2):
                            nc.tensor.transpose(bank[:, 2 * w + e, :], words[:, w, e, b, :], identity[:])
                else:
                    for s in range(2):
                        for w in range(2):
                            run = apart[k][:, 2 * b + s, 256 * w:256 * (w + 1)]
                            nc.tensor.transpose(bank[:, 2 * s + w, :], run.bitcast(F32), identity[:])

        def regroup(k):
            unit = UNITS[k]
            tag = "grouped%d" % (k % GROUPED_BUFS)
            grouped[k] = rotating.tile([P, UNIT // 2], F32, name=tag, tag=tag, align_bytes=64)
            for b in range(BANKS):
                dst = grouped[k][:, 512 * b:512 * (b + 1)]
                bank = transposed[k][b][:]
                if unit[0] == "x":
                    copy(
                        b == BANKS - 1,
                        dst.bitcast(BF16).rearrange("p (t r v) -> p t r v", t=2, v=4),
                        bank.bitcast(BF16).rearrange("p v (r t) -> p t r v", t=2),
                    )
                else:
                    copy(
                        False,
                        dst.rearrange("p (s r w) -> p s r w", s=2, w=2),
                        bank.rearrange("p (s w) r -> p s r w", w=2),
                    )

        def quantise(k):
            unit = UNITS[k]
            for lo, hi in ((0, 512), (512, 768)):
                nc.vector.quantize_mx(
                    out=codes[unit][:, lo:hi].bitcast(FP8X4),
                    scales=scales[unit][:, lo:hi],
                    in_=grouped[k][:, 2 * lo:2 * hi].bitcast(BF16),
                )

        def operand(unit, sixth):
            cols = slice(P * sixth, P * (sixth + 1))
            return codes[unit][:, cols].bitcast(FP8X4), scales[unit][:, cols]

        def multiply(i, j):
            tag = "product%d" % ((ROW_TILES * j + i) % PRODUCT_BANKS)
            product[(i, j)] = psum.tile([P, GROUPS, P], F32, name=tag, tag=tag)
            passes = [(t, h) for t in range(TAPS) for h in range(HALVES)]
            for g in range(GROUPS):
                for t, h in passes:
                    if t < 2:
                        a_codes, a_scales = operand(("x", i, h), 2 * g + t)
                    else:
                        a_codes, a_scales = operand(("q2", i, 0), HALVES * g + h)
                    w_codes, w_scales = operand(("w", j, 0), HALVES * t + h)
                    nc.tensor.matmul_mx(
                        out=product[(i, j)][:, g, :],
                        lhsT=a_codes,
                        lhsT_scale=a_scales,
                        rhs=w_codes,
                        rhs_scale=w_scales,
                        start=(t, h) == passes[0],
                        stop=(t, h) == passes[-1],
                    )

        def residual_plus_bias(j):
            nc.vector.tensor_tensor(
                out=result[j][:].rearrange("p i (o g) -> p i o g", g=GROUPS),
                in0=q1_loaded[:, :, GROUPS * P * j:GROUPS * P * (j + 1)].rearrange("p i (o g) -> p i o g", g=GROUPS),
                in1=bias[:, P * j:P * (j + 1)].unsqueeze(1).unsqueeze(3).to_broadcast([P, ROW_TILES, P, GROUPS]),
                op=ADD,
            )

        def add_product(i, j):
            view = result[j][:, i, :].rearrange("p (o g) -> p o g", g=GROUPS)
            nc.vector.tensor_tensor(out=view, in0=product[(i, j)][:].rearrange("p g o -> p o g"), in1=view, op=ADD)

        def relu_and_store(i, j):
            nc.scalar.activation(out=result[j][:, i, :], in_=result[j][:, i, :], func=RELU)
            nc.sync.dma_start(
                out=out[rows(i), P * j:P * (j + 1), :].rearrange("n o g -> n (o g)"), in_=result[j][:, i, :]
            )

        for step in range(len(UNITS) + 3):
            multiplied = step - 2 - FIRST_W
            finished = multiplied - 1
            if 0 <= step - 2 < len(UNITS):
                quantise(step - 2)
            if 0 <= finished < W_TILES:
                for i in range(ROW_TILES):
                    add_product(i, finished)
            if step < len(UNITS):
                set_taps_apart(step)
            if 0 <= step - 1 < len(UNITS):
                transpose(step - 1)
            if 0 <= multiplied < W_TILES:
                for i in range(ROW_TILES):
                    multiply(i, multiplied)
                residual_plus_bias(multiplied)
            if 0 <= step - 1 < len(UNITS):
                regroup(step - 1)
            if 0 <= finished < W_TILES:
                for i in range(ROW_TILES):
                    relu_and_store(i, finished)
